import numpy as np
import ml_dtypes


def mxq(x, axis, fmt="e4m3"):
    dtype, down = {"e4m3": (ml_dtypes.float8_e4m3fn, 7), "e5m2": (ml_dtypes.float8_e5m2, 14)}[fmt]
    v = np.moveaxis(np.asarray(x, np.float32).astype(ml_dtypes.bfloat16).astype(np.float64), axis, -1)
    blocks = v.reshape(v.shape[:-1] + (-1, 32))
    amax = np.abs(blocks).max(-1, keepdims=True)
    byte = np.maximum(np.where(amax > 0, np.frexp(amax)[1] - 1 + 127, 0) - down, 1)
    scale = np.exp2(byte - 127.0)
    codes = (blocks / scale).astype(np.float32).astype(dtype).astype(np.float64)
    return np.moveaxis((codes * scale).reshape(v.shape), -1, axis)


WIDE = False


def mx_kscale(k):
    if not WIDE:
        return np.ones(k)
    levels = np.array([10, -10, 5, -5, 0])
    a = np.random.permutation(np.resize(levels, k // 512 * 4)).reshape(k // 512, 4)
    idx = np.arange(k)
    return np.exp2(a[idx // 512, idx % 128 // 32])


BF16 = ml_dtypes.bfloat16


def bf(x):
    return np.asarray(x, np.float32).astype(BF16)


def f64(x):
    return np.asarray(x).astype(np.float64)


B, G, DB, DR = 4096, 4, 512, 512


def mish(v):
    return v * np.tanh(np.log(1.0 + np.exp(v)))


def setup_inputs():
    s, t = mx_kscale(DR), mx_kscale(DB)
    return {"BB_feature": bf(np.random.standard_normal((B, G, DB)) * t),
            "RF_feature": bf(np.random.standard_normal((B, DR)) * s),
            "W_rfrf": bf(np.random.standard_normal((DR, DR)) / np.sqrt(DR) / s),
            "b_rfrf": bf(np.random.standard_normal(DR) * 0.5),
            "W_bbrf": bf(np.random.standard_normal((DR, DB)) * np.sqrt(G / DB) / t),
            "b_bbrf": bf(np.random.standard_normal(DR) * 0.5)}


def reference(BB_feature, RF_feature, W_rfrf, b_rfrf, W_bbrf, b_bbrf):
    BB_mean = np.mean(f64(BB_feature), axis=-2)
    RF_to_RF = mish((mxq(f64(RF_feature), 1, "e4m3") @ mxq(f64(W_rfrf), 1, "e4m3").T) + f64(b_rfrf))
    BB_to_RF = mish((mxq(BB_mean, 1, "e4m3") @ mxq(f64(W_bbrf), 1, "e4m3").T) + f64(b_bbrf))
    return RF_to_RF + BB_to_RF

@@ -1,0 +1,263 @@
+import concourse.mybir as mybir
+from concourse.masks import make_identity
+
+F32 = mybir.dt.float32
+BF16 = mybir.dt.bfloat16
+U32 = mybir.dt.uint32
+U8 = mybir.dt.uint8
+FP8X4 = mybir.dt.float8_e4m3fn_x4
+ACT = mybir.ActivationFunctionType
+ALU = mybir.AluOpType
+
+P = 128
+PACK = 4
+ROWS = 4096
+GROUPS = 4
+K = 512
+N_OUT = 512
+BLOCK = 512
+BLOCKS = ROWS // BLOCK
+SLABS = BLOCK // P
+CHUNKS = N_OUT // P
+BATCH = 2
+BATCHES = BLOCKS // BATCH
+RF = 0
+BB = 1
+BRANCHES = (RF, BB)
+PER_PIECE = P // GROUPS
+PIECES = P // PER_PIECE
+TENSOR_SLABS = 3
+TINY = 1e-18
+
+FLOPS = 2 * 2 * ROWS * K * N_OUT
+
+
+def tile_gnn_layer_pa_t_kernel(tc, BB_feature, RF_feature, W_rfrf, b_rfrf, W_bbrf, b_bbrf, out):
+    nc = tc.nc
+    bb_rows = BB_feature.rearrange("b g k -> (b g) k")
+
+    with tc.manual_schedule(), tc.tile_pool(name="const", bufs=1) as const, tc.tile_pool(
+        name="loads", bufs=3
+    ) as loads, tc.tile_pool(name="sums", bufs=2) as sums, tc.tile_pool(
+        name="regroup", bufs=2
+    ) as regroup, tc.tile_pool(name="stage", bufs=2 * BATCH * CHUNKS) as stage, tc.tile_pool(
+        name="result", bufs=2
+    ) as result, tc.psum_pool(name="front", bufs=2) as front, tc.psum_pool(
+        name="first", bufs=2
+    ) as first, tc.psum_pool(name="again", bufs=2) as again, tc.psum_pool(name="back", bufs=2) as back:
+        ident_f32 = const.tile([P, P], F32)
+        make_identity(nc, ident_f32[:])
+        ident_bf16 = const.tile([P, P], BF16)
+        make_identity(nc, ident_bf16[:])
+        group_ones_f32 = const.tile([P, PER_PIECE], F32)
+        nc.vector.tensor_reduce(
+            out=group_ones_f32[:],
+            in_=ident_f32[:].rearrange("p (c g) -> p c g", g=GROUPS),
+            axis=mybir.AxisListType.X,
+            op=ALU.add,
+        )
+        group_ones = const.tile([P, PER_PIECE], BF16)
+        nc.vector.tensor_copy(out=group_ones[:], in_=group_ones_f32[:])
+        tiny = const.tile([P, 1], F32)
+        nc.vector.memset(tiny[:], TINY)
+
+        w_codes = [const.tile([P, N_OUT], U32, name="w_codes%d" % br, align_bytes=64) for br in BRANCHES]
+        w_scales = [const.tile([P, N_OUT], U8, name="w_scales%d" % br, align_bytes=64) for br in BRANCHES]
+        x_codes = [const.tile([P, ROWS], U32, name="x_codes%d" % br, align_bytes=64) for br in BRANCHES]
+        x_scales = [const.tile([P, ROWS], U8, name="x_scales%d" % br, align_bytes=64) for br in BRANCHES]
+
+        loaded = {}
+
+        def load_rows(pool, dram_rows, name):
+            rows = pool.tile([P, SLABS, K], BF16, name=name)
+            nc.sync.dma_start(out=rows[:], in_=dram_rows.rearrange("(s p) k -> p s k", p=P))
+            return rows
+
+        def load_block(blk):
+            rf = load_rows(loads, RF_feature[blk * BLOCK : (blk + 1) * BLOCK, :], "rf_rows")
+            stacked = loads.tile([P, TENSOR_SLABS * PIECES, K], BF16)
+            row0 = blk * BLOCK * GROUPS
+            nc.sync.dma_start(
+                out=stacked[:],
+                in_=bb_rows[row0 : row0 + TENSOR_SLABS * P * GROUPS, :].rearrange("(i p) k -> p i k", p=P),
+            )
+            wide = loads.tile([P, GROUPS, K], BF16)
+            nc.sync.dma_start(out=wide[:], in_=BB_feature[blk * BLOCK + TENSOR_SLABS * P : (blk + 1) * BLOCK, :, :])
+            loaded[blk] = (rf, stacked, wide)
+
+        def regroup_by_words(rows):
+            words = rows[:].bitcast(F32)
+            grouped = regroup.tile([P, BLOCK, PACK], BF16, align_bytes=64)
+            grouped_words = grouped[:].bitcast(F32)
+            for half in range(SLABS // 2):
+                bank = front.tile([P, 2, 2, P], F32, tag="front")
+                for s in range(2):
+                    for u in range(2):
+                        nc.tensor.transpose(bank[:, s, u, :], words[:, 2 * half + s, u * P : (u + 1) * P], ident_f32[:])
+                nc.vector.tensor_copy(
+                    out=grouped_words[:, 2 * half * P : 2 * (half + 1) * P, :].rearrange("p (s r) u -> p s r u", s=2),
+                    in_=bank[:].rearrange("p s u r -> p s r u"),
+                )
+            return grouped
+
+        def regroup_weights_by_quarters(rows):
+            grouped = regroup.tile([P, BLOCK, PACK], BF16, align_bytes=64)
+            for s in range(SLABS):
+                bank = front.tile([P, PACK, P], BF16, tag="front")
+                for t in range(PACK):
+                    nc.tensor.transpose(bank[:, t, :], rows[:, s, t * P : (t + 1) * P], ident_bf16[:])
+                nc.vector.tensor_copy(out=grouped[:, s * P : (s + 1) * P, :], in_=bank[:].rearrange("p t r -> p r t"))
+            return grouped
+
+        def regroup_mean(stacked, wide):
+            pair01 = sums.tile([P, K], F32)
+            nc.gpsimd.tensor_tensor(out=pair01[:], in0=wide[:, 0, :], in1=wide[:, 1, :], op=ALU.add)
+            pair23 = sums.tile([P, K], F32)
+            nc.gpsimd.tensor_tensor(out=pair23[:], in0=wide[:, 2, :], in1=wide[:, 3, :], op=ALU.add)
+            nc.gpsimd.tensor_tensor(out=pair01[:], in0=pair01[:], in1=pair23[:], op=ALU.add)
+
+            grouped = regroup.tile([P, BLOCK, PACK], BF16, align_bytes=64)
+            for s in range(SLABS):
+                bank = front.tile([P, PACK, P], F32, tag="front")
+                if s < TENSOR_SLABS:
+                    for i in range(PIECES):
+                        for t in range(PACK):
+                            nc.tensor.matmul(
+                                bank[:, t, i * PER_PIECE : (i + 1) * PER_PIECE],
+                                lhsT=stacked[:, s * PIECES + i, t * P : (t + 1) * P],
+                                rhs=group_ones[:],
+                                start=True,
+                                stop=True,
+                            )
+                else:
+                    for t in range(PACK):
+                        nc.tensor.transpose(bank[:, t, :], pair01[:, t * P : (t + 1) * P], ident_f32[:])
+                nc.vector.tensor_scalar(
+                    out=grouped[:, s * P : (s + 1) * P, :],
+                    in0=bank[:].rearrange("p t r -> p r t"),
+                    scalar1=1.0 / GROUPS,
+                    scalar2=None,
+                    op0=ALU.mult,
+                )
+            return grouped
+
+        def quantise(grouped, codes, scales):
+            nc.vector.quantize_mx(
+                out=codes.bitcast(FP8X4), scales=scales, in_=grouped[:].rearrange("p c t -> p (c t)")
+            )
+
+        def prepare_block(blk):
+            if blk + 2 < BLOCKS:
+                load_block(blk + 2)
+            rf, stacked, wide = loaded[blk]
+            cols = slice(blk * BLOCK, (blk + 1) * BLOCK)
+            grouped_rf = regroup_by_words(rf)
+            grouped_bb = regroup_mean(stacked, wide)
+            quantise(grouped_rf, x_codes[RF][:, cols], x_scales[RF][:, cols])
+            quantise(grouped_bb, x_codes[BB][:, cols], x_scales[BB][:, cols])
+
+        def product(pool, blk, chunk, br):
+            acc = pool.tile([P, BLOCK], F32)
+            n_cols = slice(chunk * P, (chunk + 1) * P)
+            b_cols = slice(blk * BLOCK, (blk + 1) * BLOCK)
+            nc.tensor.matmul_mx(
+                out=acc[:],
+                lhsT=w_codes[br][:, n_cols].bitcast(FP8X4),
+                lhsT_scale=w_scales[br][:, n_cols],
+                rhs=x_codes[br][:, b_cols].bitcast(FP8X4),
+                rhs_scale=x_scales[br][:, b_cols],
+                start=True,
+                stop=True,
+            )
+            return acc
+
+        staged = {}
+
+        def sigmoid_step(blk, chunk, br):
+            if br == RF:
+                both = stage.tile([P, 2, BLOCK], F32)
+                staged[(blk, chunk)] = both
+            acc = product(first, blk, chunk, br)
+            col = br * CHUNKS + chunk
+            nc.scalar.activation(
+                out=staged[(blk, chunk)][:, br, :], in_=acc[:], func=ACT.Sigmoid, bias=bias_neg[:, col : col + 1], scale=-1.0
+            )
+
+        def log_step(blk, chunk):
+            flat = staged[(blk, chunk)][:].rearrange("p a b -> p (a b)")
+            nc.scalar.activation(out=flat, in_=flat, func=ACT.Ln, bias=tiny[:, 0:1], scale=1.0)
+
+        def mish_step(blk, chunk, br):
+            half = staged[(blk, chunk)][:, br, :]
+            nc.scalar.activation(out=half, in_=half, func=ACT.Tanh, scale=-1.0)
+            acc = product(again, blk, chunk, br)
+            col = br * CHUNKS + chunk
+            nc.vector.scalar_tensor_tensor(
+                out=half, in0=acc[:], scalar=bias_pos[:, col : col + 1], in1=half, op0=ALU.add, op1=ALU.mult
+            )
+
+        def add_branches(blk, chunk):
+            both = staged[(blk, chunk)]
+            nc.gpsimd.tensor_tensor(out=both[:, RF, :], in0=both[:, RF, :], in1=both[:, BB, :], op=ALU.add)
+
+        finished = {}
+
+        def transpose_back(blk, chunk):
+            if chunk == 0:
+                rows_out = result.tile([P, SLABS, N_OUT], F32)
+                finished[blk] = rows_out
+            bank = back.tile([P, SLABS, P], F32)
+            for s in range(SLABS):
+                nc.tensor.transpose(bank[:, s, :], staged[(blk, chunk)][:, RF, s * P : (s + 1) * P], ident_f32[:])
+            nc.vector.tensor_copy(out=finished[blk][:, :, chunk * P : (chunk + 1) * P], in_=bank[:])
+            if chunk == CHUNKS - 1:
+                nc.sync.dma_start(
+                    out=out[blk * BLOCK : (blk + 1) * BLOCK, :].rearrange("(s p) n -> p s n", p=P), in_=finished[blk][:]
+                )
+
+        bias_rows = const.tile([P, P], BF16)
+        nc.vector.memset(bias_rows[:], 0.0)
+        nc.sync.dma_start(out=bias_rows[0:CHUNKS, :], in_=b_rfrf.rearrange("(c p) -> c p", p=P))
+        nc.sync.dma_start(out=bias_rows[CHUNKS : 2 * CHUNKS, :], in_=b_bbrf.rearrange("(c p) -> c p", p=P))
+        w_rf_rows = load_rows(const, W_rfrf, "w_rf_rows")
+        w_bb_rows = load_rows(const, W_bbrf, "w_bb_rows")
+        load_block(0)
+        load_block(1)
+        bias_bank = front.tile([P, P], BF16, tag="front")
+        nc.tensor.transpose(bias_bank[:], bias_rows[:], ident_bf16[:])
+        bias_pos = const.tile([P, 2 * CHUNKS], F32)
+        nc.vector.tensor_copy(out=bias_pos[:], in_=bias_bank[:, 0 : 2 * CHUNKS])
+        bias_neg = const.tile([P, 2 * CHUNKS], F32)
+        nc.vector.tensor_scalar(
+            out=bias_neg[:], in0=bias_bank[:, 0 : 2 * CHUNKS], scalar1=-1.0, scalar2=None, op0=ALU.mult
+        )
+
+        grouped_w_rf = regroup_by_words(w_rf_rows)
+        grouped_w_bb = regroup_weights_by_quarters(w_bb_rows)
+        quantise(grouped_w_rf, w_codes[RF][:], w_scales[RF][:])
+        quantise(grouped_w_bb, w_codes[BB][:], w_scales[BB][:])
+
+        for blk in range(BATCH):
+            prepare_block(blk)
+        for blk in range(BATCH):
+            for chunk in range(CHUNKS):
+                for br in BRANCHES:
+                    sigmoid_step(blk, chunk, br)
+
+        for batch in range(BATCHES):
+            steps = [(blk, chunk) for blk in range(batch * BATCH, (batch + 1) * BATCH) for chunk in range(CHUNKS)]
+            more = batch + 1 < BATCHES
+            for blk, chunk in steps:
+                log_step(blk, chunk)
+            if more:
+                for blk in range((batch + 1) * BATCH, (batch + 2) * BATCH):
+                    prepare_block(blk)
+            for i, (blk, chunk) in enumerate(steps):
+                for br in BRANCHES:
+                    if more:
+                        sigmoid_step(blk + BATCH, chunk, br)
+                    mish_step(blk, chunk, br)
+                add_branches(blk, chunk)
+                if i > 0:
+                    transpose_back(*steps[i - 1])
+            transpose_back(*steps[-1])

@@ -19,8 +19,11 @@ BLOCK = 512
 BLOCKS = ROWS // BLOCK
 SLABS = BLOCK // P
 CHUNKS = N_OUT // P
-BATCH = 2
+BATCH = 4
 BATCHES = BLOCKS // BATCH
+STEPS = BATCH * CHUNKS
+BEHIND = 2
+AHEAD = 2
 RF = 0
 BB = 1
 BRANCHES = (RF, BB)
@@ -37,14 +40,16 @@ def tile_gnn_layer_pa_t_kernel(tc, BB_feature, RF_feature, W_rfrf, b_rfrf, W_bbr
     bb_rows = BB_feature.rearrange("b g k -> (b g) k")
 
     with tc.manual_schedule(), tc.tile_pool(name="const", bufs=1) as const, tc.tile_pool(
-        name="loads", bufs=3
-    ) as loads, tc.tile_pool(name="sums", bufs=2) as sums, tc.tile_pool(
-        name="regroup", bufs=2
-    ) as regroup, tc.tile_pool(name="stage", bufs=2 * BATCH * CHUNKS) as stage, tc.tile_pool(
-        name="result", bufs=2
+        name="rf_loads", bufs=AHEAD + 3
+    ) as rf_loads, tc.tile_pool(name="bb_loads", bufs=AHEAD + 1) as bb_loads, tc.tile_pool(
+        name="sums", bufs=AHEAD + 2
+    ) as sums, tc.tile_pool(name="regroup", bufs=2) as regroup, tc.tile_pool(
+        name="stage", bufs=STEPS + 2 * BEHIND
+    ) as stage, tc.tile_pool(
+        name="result", bufs=4
     ) as result, tc.psum_pool(name="front", bufs=2) as front, tc.psum_pool(
-        name="first", bufs=2
-    ) as first, tc.psum_pool(name="again", bufs=2) as again, tc.psum_pool(name="back", bufs=2) as back:
+        name="products", bufs=4
+    ) as products, tc.psum_pool(name="back", bufs=2) as back:
         ident_f32 = const.tile([P, P], F32)
         make_identity(nc, ident_f32[:])
         ident_bf16 = const.tile([P, P], BF16)
@@ -66,24 +71,30 @@ def tile_gnn_layer_pa_t_kernel(tc, BB_feature, RF_feature, W_rfrf, b_rfrf, W_bbr
         x_codes = [const.tile([P, ROWS], U32, name="x_codes%d" % br, align_bytes=64) for br in BRANCHES]
         x_scales = [const.tile([P, ROWS], U8, name="x_scales%d" % br, align_bytes=64) for br in BRANCHES]
 
-        loaded = {}
+        loaded_rf = {}
+        loaded_bb = {}
 
-        def load_rows(pool, dram_rows, name):
-            rows = pool.tile([P, SLABS, K], BF16, name=name)
+        def load_rows(dram_rows):
+            rows = rf_loads.tile([P, SLABS, K], BF16)
             nc.sync.dma_start(out=rows[:], in_=dram_rows.rearrange("(s p) k -> p s k", p=P))
             return rows
 
         def load_block(blk):
-            rf = load_rows(loads, RF_feature[blk * BLOCK : (blk + 1) * BLOCK, :], "rf_rows")
-            stacked = loads.tile([P, TENSOR_SLABS * PIECES, K], BF16)
+            loaded_rf[blk] = load_rows(RF_feature[blk * BLOCK : (blk + 1) * BLOCK, :])
+            wide = bb_loads.tile([P, GROUPS, K], BF16)
+            nc.sync.dma_start(out=wide[:], in_=BB_feature[blk * BLOCK + TENSOR_SLABS * P : (blk + 1) * BLOCK, :, :])
+            pair01 = sums.tile([P, K], F32)
+            nc.gpsimd.tensor_tensor(out=pair01[:], in0=wide[:, 0, :], in1=wide[:, 1, :], op=ALU.add)
+            pair23 = sums.tile([P, K], F32, bufs=2)
+            nc.gpsimd.tensor_tensor(out=pair23[:], in0=wide[:, 2, :], in1=wide[:, 3, :], op=ALU.add)
+            nc.gpsimd.tensor_tensor(out=pair01[:], in0=pair01[:], in1=pair23[:], op=ALU.add)
+            stacked = bb_loads.tile([P, TENSOR_SLABS * PIECES, K], BF16)
             row0 = blk * BLOCK * GROUPS
             nc.sync.dma_start(
                 out=stacked[:],
                 in_=bb_rows[row0 : row0 + TENSOR_SLABS * P * GROUPS, :].rearrange("(i p) k -> p i k", p=P),
             )
-            wide = loads.tile([P, GROUPS, K], BF16)
-            nc.sync.dma_start(out=wide[:], in_=BB_feature[blk * BLOCK + TENSOR_SLABS * P : (blk + 1) * BLOCK, :, :])
-            loaded[blk] = (rf, stacked, wide)
+            loaded_bb[blk] = (stacked, pair01)
 
         def regroup_by_words(rows):
             words = rows[:].bitcast(F32)
@@ -109,55 +120,53 @@ def tile_gnn_layer_pa_t_kernel(tc, BB_feature, RF_feature, W_rfrf, b_rfrf, W_bbr
                 nc.vector.tensor_copy(out=grouped[:, s * P : (s + 1) * P, :], in_=bank[:].rearrange("p t r -> p r t"))
             return grouped
 
-        def regroup_mean(stacked, wide):
-            pair01 = sums.tile([P, K], F32)
-            nc.gpsimd.tensor_tensor(out=pair01[:], in0=wide[:, 0, :], in1=wide[:, 1, :], op=ALU.add)
-            pair23 = sums.tile([P, K], F32)
-            nc.gpsimd.tensor_tensor(out=pair23[:], in0=wide[:, 2, :], in1=wide[:, 3, :], op=ALU.add)
-            nc.gpsimd.tensor_tensor(out=pair01[:], in0=pair01[:], in1=pair23[:], op=ALU.add)
-
-            grouped = regroup.tile([P, BLOCK, PACK], BF16, align_bytes=64)
-            for s in range(SLABS):
-                bank = front.tile([P, PACK, P], F32, tag="front")
-                if s < TENSOR_SLABS:
-                    for i in range(PIECES):
-                        for t in range(PACK):
-                            nc.tensor.matmul(
-                                bank[:, t, i * PER_PIECE : (i + 1) * PER_PIECE],
-                                lhsT=stacked[:, s * PIECES + i, t * P : (t + 1) * P],
-                                rhs=group_ones[:],
-                                start=True,
-                                stop=True,
-                            )
-                else:
+        def regroup_mean_slab(grouped, stacked, last_slab_sum, s):
+            bank = front.tile([P, PACK, P], F32, tag="front")
+            if s < TENSOR_SLABS:
+                for i in range(PIECES):
                     for t in range(PACK):
-                        nc.tensor.transpose(bank[:, t, :], pair01[:, t * P : (t + 1) * P], ident_f32[:])
-                nc.vector.tensor_scalar(
-                    out=grouped[:, s * P : (s + 1) * P, :],
-                    in0=bank[:].rearrange("p t r -> p r t"),
-                    scalar1=1.0 / GROUPS,
-                    scalar2=None,
-                    op0=ALU.mult,
-                )
-            return grouped
+                        nc.tensor.matmul(
+                            bank[:, t, i * PER_PIECE : (i + 1) * PER_PIECE],
+                            lhsT=stacked[:, s * PIECES + i, t * P : (t + 1) * P],
+                            rhs=group_ones[:],
+                            start=True,
+                            stop=True,
+                        )
+            else:
+                for t in range(PACK):
+                    nc.tensor.transpose(bank[:, t, :], last_slab_sum[:, t * P : (t + 1) * P], ident_f32[:])
+            nc.vector.tensor_scalar(
+                out=grouped[:, s * P : (s + 1) * P, :],
+                in0=bank[:].rearrange("p t r -> p r t"),
+                scalar1=1.0 / GROUPS,
+                scalar2=None,
+                op0=ALU.mult,
+            )
 
         def quantise(grouped, codes, scales):
             nc.vector.quantize_mx(
                 out=codes.bitcast(FP8X4), scales=scales, in_=grouped[:].rearrange("p c t -> p (c t)")
             )
 
-        def prepare_block(blk):
-            if blk + 2 < BLOCKS:
-                load_block(blk + 2)
-            rf, stacked, wide = loaded[blk]
+        def prepare_rf(blk):
             cols = slice(blk * BLOCK, (blk + 1) * BLOCK)
-            grouped_rf = regroup_by_words(rf)
-            grouped_bb = regroup_mean(stacked, wide)
-            quantise(grouped_rf, x_codes[RF][:, cols], x_scales[RF][:, cols])
-            quantise(grouped_bb, x_codes[BB][:, cols], x_scales[BB][:, cols])
+            quantise(regroup_by_words(loaded_rf[blk]), x_codes[RF][:, cols], x_scales[RF][:, cols])
 
-        def product(pool, blk, chunk, br):
-            acc = pool.tile([P, BLOCK], F32)
+        grouped_means = {}
+
+        def prepare_bb_slab(blk, s):
+            if s == 0:
+                grouped = regroup.tile([P, BLOCK, PACK], BF16, align_bytes=64)
+                grouped_means[blk] = grouped
+            regroup_mean_slab(grouped_means[blk], *loaded_bb[blk], s)
+            if s == SLABS - 1:
+                cols = slice(blk * BLOCK, (blk + 1) * BLOCK)
+                quantise(grouped_means[blk], x_codes[BB][:, cols], x_scales[BB][:, cols])
+                if blk + AHEAD < BLOCKS:
+                    load_block(blk + AHEAD)
+
+        def product(blk, chunk, br):
+            acc = products.tile([P, BLOCK], F32)
             n_cols = slice(chunk * P, (chunk + 1) * P)
             b_cols = slice(blk * BLOCK, (blk + 1) * BLOCK)
             nc.tensor.matmul_mx(
@@ -177,7 +186,7 @@ def tile_gnn_layer_pa_t_kernel(tc, BB_feature, RF_feature, W_rfrf, b_rfrf, W_bbr
             if br == RF:
                 both = stage.tile([P, 2, BLOCK], F32)
                 staged[(blk, chunk)] = both
-            acc = product(first, blk, chunk, br)
+            acc = product(blk, chunk, br)
             col = br * CHUNKS + chunk
             nc.scalar.activation(
                 out=staged[(blk, chunk)][:, br, :], in_=acc[:], func=ACT.Sigmoid, bias=bias_neg[:, col : col + 1], scale=-1.0
@@ -187,10 +196,13 @@ def tile_gnn_layer_pa_t_kernel(tc, BB_feature, RF_feature, W_rfrf, b_rfrf, W_bbr
             flat = staged[(blk, chunk)][:].rearrange("p a b -> p (a b)")
             nc.scalar.activation(out=flat, in_=flat, func=ACT.Ln, bias=tiny[:, 0:1], scale=1.0)
 
+        def tanh_step(blk, chunk):
+            flat = staged[(blk, chunk)][:].rearrange("p a b -> p (a b)")
+            nc.scalar.activation(out=flat, in_=flat, func=ACT.Tanh, scale=-1.0)
+
         def mish_step(blk, chunk, br):
             half = staged[(blk, chunk)][:, br, :]
-            nc.scalar.activation(out=half, in_=half, func=ACT.Tanh, scale=-1.0)
-            acc = product(again, blk, chunk, br)
+            acc = product(blk, chunk, br)
             col = br * CHUNKS + chunk
             nc.vector.scalar_tensor_tensor(
                 out=half, in0=acc[:], scalar=bias_pos[:, col : col + 1], in1=half, op0=ALU.add, op1=ALU.mult
@@ -200,29 +212,28 @@ def tile_gnn_layer_pa_t_kernel(tc, BB_feature, RF_feature, W_rfrf, b_rfrf, W_bbr
             both = staged[(blk, chunk)]
             nc.gpsimd.tensor_tensor(out=both[:, RF, :], in0=both[:, RF, :], in1=both[:, BB, :], op=ALU.add)
 
-        finished = {}
-
-        def transpose_back(blk, chunk):
-            if chunk == 0:
-                rows_out = result.tile([P, SLABS, N_OUT], F32)
-                finished[blk] = rows_out
+        def transpose_back(blk, chunk, on_scalar):
             bank = back.tile([P, SLABS, P], F32)
             for s in range(SLABS):
                 nc.tensor.transpose(bank[:, s, :], staged[(blk, chunk)][:, RF, s * P : (s + 1) * P], ident_f32[:])
-            nc.vector.tensor_copy(out=finished[blk][:, :, chunk * P : (chunk + 1) * P], in_=bank[:])
-            if chunk == CHUNKS - 1:
-                nc.sync.dma_start(
-                    out=out[blk * BLOCK : (blk + 1) * BLOCK, :].rearrange("(s p) n -> p s n", p=P), in_=finished[blk][:]
-                )
+            piece = result.tile([P, SLABS, P], F32)
+            if on_scalar:
+                nc.scalar.copy(out=piece[:], in_=bank[:])
+            else:
+                nc.vector.tensor_copy(out=piece[:], in_=bank[:])
+            nc.sync.dma_start(
+                out=out[blk * BLOCK : (blk + 1) * BLOCK, chunk * P : (chunk + 1) * P].rearrange("(s p) n -> p s n", p=P),
+                in_=piece[:],
+            )
 
         bias_rows = const.tile([P, P], BF16)
         nc.vector.memset(bias_rows[:], 0.0)
         nc.sync.dma_start(out=bias_rows[0:CHUNKS, :], in_=b_rfrf.rearrange("(c p) -> c p", p=P))
         nc.sync.dma_start(out=bias_rows[CHUNKS : 2 * CHUNKS, :], in_=b_bbrf.rearrange("(c p) -> c p", p=P))
-        w_rf_rows = load_rows(const, W_rfrf, "w_rf_rows")
-        w_bb_rows = load_rows(const, W_bbrf, "w_bb_rows")
-        load_block(0)
-        load_block(1)
+        w_rf_rows = load_rows(W_rfrf)
+        w_bb_rows = load_rows(W_bbrf)
+        for blk in range(AHEAD):
+            load_block(blk)
         bias_bank = front.tile([P, P], BF16, tag="front")
         nc.tensor.transpose(bias_bank[:], bias_rows[:], ident_bf16[:])
         bias_pos = const.tile([P, 2 * CHUNKS], F32)
@@ -232,32 +243,39 @@ def tile_gnn_layer_pa_t_kernel(tc, BB_feature, RF_feature, W_rfrf, b_rfrf, W_bbr
             out=bias_neg[:], in0=bias_bank[:, 0 : 2 * CHUNKS], scalar1=-1.0, scalar2=None, op0=ALU.mult
         )
 
-        grouped_w_rf = regroup_by_words(w_rf_rows)
-        grouped_w_bb = regroup_weights_by_quarters(w_bb_rows)
-        quantise(grouped_w_rf, w_codes[RF][:], w_scales[RF][:])
-        quantise(grouped_w_bb, w_codes[BB][:], w_scales[BB][:])
+        quantise(regroup_by_words(w_rf_rows), w_codes[RF][:], w_scales[RF][:])
+        quantise(regroup_weights_by_quarters(w_bb_rows), w_codes[BB][:], w_scales[BB][:])
 
-        for blk in range(BATCH):
-            prepare_block(blk)
-        for blk in range(BATCH):
+        for blk in range(BATCH + 1):
+            if blk < BATCH:
+                prepare_rf(blk)
             for chunk in range(CHUNKS):
-                for br in BRANCHES:
-                    sigmoid_step(blk, chunk, br)
+                if blk < BATCH:
+                    sigmoid_step(blk, chunk, RF)
+                    prepare_bb_slab(blk, chunk)
+                if blk > 0:
+                    sigmoid_step(blk - 1, chunk, BB)
 
+        all_steps = [(blk, chunk) for blk in range(BLOCKS) for chunk in range(CHUNKS)]
         for batch in range(BATCHES):
-            steps = [(blk, chunk) for blk in range(batch * BATCH, (batch + 1) * BATCH) for chunk in range(CHUNKS)]
             more = batch + 1 < BATCHES
-            for blk, chunk in steps:
+            for blk, chunk in all_steps[batch * STEPS : (batch + 1) * STEPS]:
                 log_step(blk, chunk)
             if more:
                 for blk in range((batch + 1) * BATCH, (batch + 2) * BATCH):
-                    prepare_block(blk)
-            for i, (blk, chunk) in enumerate(steps):
-                for br in BRANCHES:
-                    if more:
+                    prepare_rf(blk)
+                    for s in range(SLABS):
+                        prepare_bb_slab(blk, s)
+            for i in range(batch * STEPS, (batch + 1) * STEPS):
+                blk, chunk = all_steps[i]
+                if more:
+                    for br in BRANCHES:
                         sigmoid_step(blk + BATCH, chunk, br)
+                tanh_step(blk, chunk)
+                for br in BRANCHES:
                     mish_step(blk, chunk, br)
                 add_branches(blk, chunk)
-                if i > 0:
-                    transpose_back(*steps[i - 1])
-            transpose_back(*steps[-1])
+                if i >= BEHIND:
+                    transpose_back(*all_steps[i - BEHIND], on_scalar=(not more and i % 2 == 1))
+        for i in range(len(all_steps), len(all_steps) + BEHIND):
+            transpose_back(*all_steps[i - BEHIND], on_scalar=(i % 2 == 1))

@@ -19,7 +19,7 @@ BLOCK = 512
 BLOCKS = ROWS // BLOCK
 SLABS = BLOCK // P
 CHUNKS = N_OUT // P
-BATCH = 4
+BATCH = 2
 BATCHES = BLOCKS // BATCH
 STEPS = BATCH * CHUNKS
 BEHIND = 2
@@ -44,7 +44,7 @@ def tile_gnn_layer_pa_t_kernel(tc, BB_feature, RF_feature, W_rfrf, b_rfrf, W_bbr
     ) as rf_loads, tc.tile_pool(name="bb_loads", bufs=AHEAD + 1) as bb_loads, tc.tile_pool(
         name="sums", bufs=AHEAD + 2
     ) as sums, tc.tile_pool(name="regroup", bufs=2) as regroup, tc.tile_pool(
-        name="stage", bufs=STEPS + 2 * BEHIND
+        name="stage", bufs=STEPS + 3 * BEHIND
     ) as stage, tc.tile_pool(
         name="result", bufs=4
     ) as result, tc.psum_pool(name="front", bufs=2) as front, tc.psum_pool(
@@ -266,14 +266,17 @@ def tile_gnn_layer_pa_t_kernel(tc, BB_feature, RF_feature, W_rfrf, b_rfrf, W_bbr
                     prepare_rf(blk)
                     for s in range(SLABS):
                         prepare_bb_slab(blk, s)
+            last = (batch + 1) * STEPS - 1
+            if more:
+                for br in BRANCHES:
+                    sigmoid_step(*all_steps[batch * STEPS + STEPS], br)
             for i in range(batch * STEPS, (batch + 1) * STEPS):
                 blk, chunk = all_steps[i]
-                if more:
-                    for br in BRANCHES:
-                        sigmoid_step(blk + BATCH, chunk, br)
                 tanh_step(blk, chunk)
                 for br in BRANCHES:
                     mish_step(blk, chunk, br)
+                    if more and i < last:
+                        sigmoid_step(*all_steps[i + 1 + STEPS], br)
                 add_branches(blk, chunk)
                 if i >= BEHIND:
                     transpose_back(*all_steps[i - BEHIND], on_scalar=(not more and i % 2 == 1))

@@ -22,6 +22,7 @@ CHUNKS = N_OUT // P
 BATCH = 2
 BATCHES = BLOCKS // BATCH
 STEPS = BATCH * CHUNKS
+LAG = 1
 BEHIND = 2
 AHEAD = 2
 RF = 0
@@ -44,7 +45,7 @@ def tile_gnn_layer_pa_t_kernel(tc, BB_feature, RF_feature, W_rfrf, b_rfrf, W_bbr
     ) as rf_loads, tc.tile_pool(name="bb_loads", bufs=AHEAD + 1) as bb_loads, tc.tile_pool(
         name="sums", bufs=AHEAD + 2
     ) as sums, tc.tile_pool(name="regroup", bufs=2) as regroup, tc.tile_pool(
-        name="stage", bufs=STEPS + 3 * BEHIND
+        name="stage", bufs=2 * STEPS
     ) as stage, tc.tile_pool(
         name="result", bufs=4
     ) as result, tc.psum_pool(name="front", bufs=2) as front, tc.psum_pool(
@@ -79,8 +80,10 @@ def tile_gnn_layer_pa_t_kernel(tc, BB_feature, RF_feature, W_rfrf, b_rfrf, W_bbr
             nc.sync.dma_start(out=rows[:], in_=dram_rows.rearrange("(s p) k -> p s k", p=P))
             return rows
 
-        def load_block(blk):
+        def load_rf(blk):
             loaded_rf[blk] = load_rows(RF_feature[blk * BLOCK : (blk + 1) * BLOCK, :])
+
+        def load_bb(blk):
             wide = bb_loads.tile([P, GROUPS, K], BF16)
             nc.sync.dma_start(out=wide[:], in_=BB_feature[blk * BLOCK + TENSOR_SLABS * P : (blk + 1) * BLOCK, :, :])
             pair01 = sums.tile([P, K], F32)
@@ -88,13 +91,15 @@ def tile_gnn_layer_pa_t_kernel(tc, BB_feature, RF_feature, W_rfrf, b_rfrf, W_bbr
             pair23 = sums.tile([P, K], F32, bufs=2)
             nc.gpsimd.tensor_tensor(out=pair23[:], in0=wide[:, 2, :], in1=wide[:, 3, :], op=ALU.add)
             nc.gpsimd.tensor_tensor(out=pair01[:], in0=pair01[:], in1=pair23[:], op=ALU.add)
-            stacked = bb_loads.tile([P, TENSOR_SLABS * PIECES, K], BF16)
-            row0 = blk * BLOCK * GROUPS
-            nc.sync.dma_start(
-                out=stacked[:],
-                in_=bb_rows[row0 : row0 + TENSOR_SLABS * P * GROUPS, :].rearrange("(i p) k -> p i k", p=P),
-            )
-            loaded_bb[blk] = (stacked, pair01)
+            stacked_slabs = []
+            for s in range(TENSOR_SLABS):
+                stacked = bb_loads.tile([P, PIECES, K], BF16, bufs=(AHEAD + 1) * TENSOR_SLABS)
+                row0 = (blk * BLOCK + s * P) * GROUPS
+                nc.sync.dma_start(
+                    out=stacked[:], in_=bb_rows[row0 : row0 + P * GROUPS, :].rearrange("(i p) k -> p i k", p=P)
+                )
+                stacked_slabs.append(stacked)
+            loaded_bb[blk] = (stacked_slabs, pair01)
 
         def regroup_by_words(rows):
             words = rows[:].bitcast(F32)
@@ -120,14 +125,14 @@ def tile_gnn_layer_pa_t_kernel(tc, BB_feature, RF_feature, W_rfrf, b_rfrf, W_bbr
                 nc.vector.tensor_copy(out=grouped[:, s * P : (s + 1) * P, :], in_=bank[:].rearrange("p t r -> p r t"))
             return grouped
 
-        def regroup_mean_slab(grouped, stacked, last_slab_sum, s):
+        def regroup_mean_slab(grouped, stacked_slabs, last_slab_sum, s):
             bank = front.tile([P, PACK, P], F32, tag="front")
             if s < TENSOR_SLABS:
                 for i in range(PIECES):
                     for t in range(PACK):
                         nc.tensor.matmul(
                             bank[:, t, i * PER_PIECE : (i + 1) * PER_PIECE],
-                            lhsT=stacked[:, s * PIECES + i, t * P : (t + 1) * P],
+                            lhsT=stacked_slabs[s][:, i, t * P : (t + 1) * P],
                             rhs=group_ones[:],
                             start=True,
                             stop=True,
@@ -163,7 +168,8 @@ def tile_gnn_layer_pa_t_kernel(tc, BB_feature, RF_feature, W_rfrf, b_rfrf, W_bbr
                 cols = slice(blk * BLOCK, (blk + 1) * BLOCK)
                 quantise(grouped_means[blk], x_codes[BB][:, cols], x_scales[BB][:, cols])
                 if blk + AHEAD < BLOCKS:
-                    load_block(blk + AHEAD)
+                    load_rf(blk + AHEAD)
+                    load_bb(blk + AHEAD)
 
         def product(blk, chunk, br):
             acc = products.tile([P, BLOCK], F32)
@@ -231,9 +237,12 @@ def tile_gnn_layer_pa_t_kernel(tc, BB_feature, RF_feature, W_rfrf, b_rfrf, W_bbr
         nc.sync.dma_start(out=bias_rows[0:CHUNKS, :], in_=b_rfrf.rearrange("(c p) -> c p", p=P))
         nc.sync.dma_start(out=bias_rows[CHUNKS : 2 * CHUNKS, :], in_=b_bbrf.rearrange("(c p) -> c p", p=P))
         w_rf_rows = load_rows(W_rfrf)
+        load_rf(0)
         w_bb_rows = load_rows(W_bbrf)
-        for blk in range(AHEAD):
-            load_block(blk)
+        load_bb(0)
+        for blk in range(1, AHEAD):
+            load_rf(blk)
+            load_bb(blk)
         bias_bank = front.tile([P, P], BF16, tag="front")
         nc.tensor.transpose(bias_bank[:], bias_rows[:], ident_bf16[:])
         bias_pos = const.tile([P, 2 * CHUNKS], F32)
@@ -244,41 +253,49 @@ def tile_gnn_layer_pa_t_kernel(tc, BB_feature, RF_feature, W_rfrf, b_rfrf, W_bbr
         )
 
         quantise(regroup_by_words(w_rf_rows), w_codes[RF][:], w_scales[RF][:])
+        prepare_rf(0)
+        for chunk in range(CHUNKS):
+            sigmoid_step(0, chunk, RF)
         quantise(regroup_weights_by_quarters(w_bb_rows), w_codes[BB][:], w_scales[BB][:])
-
         for blk in range(BATCH + 1):
-            if blk < BATCH:
-                prepare_rf(blk)
+            if blk + 1 < BATCH:
+                prepare_rf(blk + 1)
             for chunk in range(CHUNKS):
                 if blk < BATCH:
-                    sigmoid_step(blk, chunk, RF)
                     prepare_bb_slab(blk, chunk)
+                if blk + 1 < BATCH:
+                    sigmoid_step(blk + 1, chunk, RF)
                 if blk > 0:
                     sigmoid_step(blk - 1, chunk, BB)
 
         all_steps = [(blk, chunk) for blk in range(BLOCKS) for chunk in range(CHUNKS)]
+
+        def trail(i, scalar_helps):
+            if 0 <= i - LAG < len(all_steps):
+                for br in BRANCHES:
+                    mish_step(*all_steps[i - LAG], br)
+                add_branches(*all_steps[i - LAG])
+            if 0 <= i - LAG - BEHIND < len(all_steps):
+                transpose_back(*all_steps[i - LAG - BEHIND], on_scalar=scalar_helps and i % 2 == 1)
+
         for batch in range(BATCHES):
             more = batch + 1 < BATCHES
-            for blk, chunk in all_steps[batch * STEPS : (batch + 1) * STEPS]:
-                log_step(blk, chunk)
+            steps = range(batch * STEPS, (batch + 1) * STEPS)
+            for i in steps:
+                log_step(*all_steps[i])
             if more:
                 for blk in range((batch + 1) * BATCH, (batch + 2) * BATCH):
                     prepare_rf(blk)
                     for s in range(SLABS):
                         prepare_bb_slab(blk, s)
-            last = (batch + 1) * STEPS - 1
             if more:
                 for br in BRANCHES:
-                    sigmoid_step(*all_steps[batch * STEPS + STEPS], br)
-            for i in range(batch * STEPS, (batch + 1) * STEPS):
-                blk, chunk = all_steps[i]
-                tanh_step(blk, chunk)
-                for br in BRANCHES:
-                    mish_step(blk, chunk, br)
-                    if more and i < last:
+                    sigmoid_step(*all_steps[steps[0] + STEPS], br)
+            for i in steps:
+                tanh_step(*all_steps[i])
+                if more and i < steps[-1]:
+                    for br in BRANCHES:
                         sigmoid_step(*all_steps[i + 1 + STEPS], br)
-                add_branches(blk, chunk)
-                if i >= BEHIND:
-                    transpose_back(*all_steps[i - BEHIND], on_scalar=(not more and i % 2 == 1))
-        for i in range(len(all_steps), len(all_steps) + BEHIND):
-            transpose_back(*all_steps[i - BEHIND], on_scalar=(i % 2 == 1))
+                trail(i, scalar_helps=not more)
+        for i in range(len(all_steps), len(all_steps) + LAG + BEHIND):
+            trail(i, scalar_helps=True)

import concourse.mybir as mybir
from concourse.masks import make_identity

F32 = mybir.dt.float32
BF16 = mybir.dt.bfloat16
U32 = mybir.dt.uint32
U8 = mybir.dt.uint8
FP8X4 = mybir.dt.float8_e4m3fn_x4
ACT = mybir.ActivationFunctionType
ALU = mybir.AluOpType

P = 128
PACK = 4
ROWS = 4096
GROUPS = 4
K = 512
N_OUT = 512
BLOCK = 512
BLOCKS = ROWS // BLOCK
SLABS = BLOCK // P
CHUNKS = N_OUT // P
BATCH = 2
BATCHES = BLOCKS // BATCH
STEPS = BATCH * CHUNKS
LAG = 1
BEHIND = 2
AHEAD = 2
RF = 0
BB = 1
BRANCHES = (RF, BB)
PER_PIECE = P // GROUPS
PIECES = P // PER_PIECE
TENSOR_SLABS = 3
TINY = 1e-18

FLOPS = 2 * 2 * ROWS * K * N_OUT


def tile_gnn_layer_pa_t_kernel(tc, BB_feature, RF_feature, W_rfrf, b_rfrf, W_bbrf, b_bbrf, out):
    nc = tc.nc
    bb_rows = BB_feature.rearrange("b g k -> (b g) k")

    with tc.manual_schedule(), tc.tile_pool(name="const", bufs=1) as const, tc.tile_pool(
        name="rf_loads", bufs=AHEAD + 3
    ) as rf_loads, tc.tile_pool(name="bb_loads", bufs=AHEAD + 1) as bb_loads, tc.tile_pool(
        name="sums", bufs=AHEAD + 2
    ) as sums, tc.tile_pool(name="regroup", bufs=2) as regroup, tc.tile_pool(
        name="stage", bufs=2 * STEPS
    ) as stage, tc.tile_pool(
        name="result", bufs=4
    ) as result, tc.psum_pool(name="front", bufs=2) as front, tc.psum_pool(
        name="products", bufs=4
    ) as products, tc.psum_pool(name="back", bufs=2) as back:
        ident_f32 = const.tile([P, P], F32)
        make_identity(nc, ident_f32[:])
        ident_bf16 = const.tile([P, P], BF16)
        make_identity(nc, ident_bf16[:])
        group_ones_f32 = const.tile([P, PER_PIECE], F32)
        nc.vector.tensor_reduce(
            out=group_ones_f32[:],
            in_=ident_f32[:].rearrange("p (c g) -> p c g", g=GROUPS),
            axis=mybir.AxisListType.X,
            op=ALU.add,
        )
        group_ones = const.tile([P, PER_PIECE], BF16)
        nc.vector.tensor_copy(out=group_ones[:], in_=group_ones_f32[:])
        tiny = const.tile([P, 1], F32)
        nc.vector.memset(tiny[:], TINY)

        w_codes = [const.tile([P, N_OUT], U32, name="w_codes%d" % br, align_bytes=64) for br in BRANCHES]
        w_scales = [const.tile([P, N_OUT], U8, name="w_scales%d" % br, align_bytes=64) for br in BRANCHES]
        x_codes = [const.tile([P, ROWS], U32, name="x_codes%d" % br, align_bytes=64) for br in BRANCHES]
        x_scales = [const.tile([P, ROWS], U8, name="x_scales%d" % br, align_bytes=64) for br in BRANCHES]

        loaded_rf = {}
        loaded_bb = {}

        def load_rows(dram_rows):
            rows = rf_loads.tile([P, SLABS, K], BF16)
            nc.sync.dma_start(out=rows[:], in_=dram_rows.rearrange("(s p) k -> p s k", p=P))
            return rows

        def load_rf(blk):
            loaded_rf[blk] = load_rows(RF_feature[blk * BLOCK : (blk + 1) * BLOCK, :])

        def load_bb(blk):
            wide = bb_loads.tile([P, GROUPS, K], BF16)
            nc.sync.dma_start(out=wide[:], in_=BB_feature[blk * BLOCK + TENSOR_SLABS * P : (blk + 1) * BLOCK, :, :])
            pair01 = sums.tile([P, K], F32)
            nc.gpsimd.tensor_tensor(out=pair01[:], in0=wide[:, 0, :], in1=wide[:, 1, :], op=ALU.add)
            pair23 = sums.tile([P, K], F32, bufs=2)
            nc.gpsimd.tensor_tensor(out=pair23[:], in0=wide[:, 2, :], in1=wide[:, 3, :], op=ALU.add)
            nc.gpsimd.tensor_tensor(out=pair01[:], in0=pair01[:], in1=pair23[:], op=ALU.add)
            stacked_slabs = []
            for s in range(TENSOR_SLABS):
                stacked = bb_loads.tile([P, PIECES, K], BF16, bufs=(AHEAD + 1) * TENSOR_SLABS)
                row0 = (blk * BLOCK + s * P) * GROUPS
                nc.sync.dma_start(
                    out=stacked[:], in_=bb_rows[row0 : row0 + P * GROUPS, :].rearrange("(i p) k -> p i k", p=P)
                )
                stacked_slabs.append(stacked)
            loaded_bb[blk] = (stacked_slabs, pair01)

        def regroup_by_words(rows):
            words = rows[:].bitcast(F32)
            grouped = regroup.tile([P, BLOCK, PACK], BF16, align_bytes=64)
            grouped_words = grouped[:].bitcast(F32)
            for half in range(SLABS // 2):
                bank = front.tile([P, 2, 2, P], F32, tag="front")
                for s in range(2):
                    for u in range(2):
                        nc.tensor.transpose(bank[:, s, u, :], words[:, 2 * half + s, u * P : (u + 1) * P], ident_f32[:])
                nc.vector.tensor_copy(
                    out=grouped_words[:, 2 * half * P : 2 * (half + 1) * P, :].rearrange("p (s r) u -> p s r u", s=2),
                    in_=bank[:].rearrange("p s u r -> p s r u"),
                )
            return grouped

        def regroup_weights_by_quarters(rows):
            grouped = regroup.tile([P, BLOCK, PACK], BF16, align_bytes=64)
            for s in range(SLABS):
                bank = front.tile([P, PACK, P], BF16, tag="front")
                for t in range(PACK):
                    nc.tensor.transpose(bank[:, t, :], rows[:, s, t * P : (t + 1) * P], ident_bf16[:])
                nc.vector.tensor_copy(out=grouped[:, s * P : (s + 1) * P, :], in_=bank[:].rearrange("p t r -> p r t"))
            return grouped

        def regroup_mean_slab(grouped, stacked_slabs, last_slab_sum, s):
            bank = front.tile([P, PACK, P], F32, tag="front")
            if s < TENSOR_SLABS:
                for i in range(PIECES):
                    for t in range(PACK):
                        nc.tensor.matmul(
                            bank[:, t, i * PER_PIECE : (i + 1) * PER_PIECE],
                            lhsT=stacked_slabs[s][:, i, t * P : (t + 1) * P],
                            rhs=group_ones[:],
                            start=True,
                            stop=True,
                        )
            else:
                for t in range(PACK):
                    nc.tensor.transpose(bank[:, t, :], last_slab_sum[:, t * P : (t + 1) * P], ident_f32[:])
            nc.vector.tensor_scalar(
                out=grouped[:, s * P : (s + 1) * P, :],
                in0=bank[:].rearrange("p t r -> p r t"),
                scalar1=1.0 / GROUPS,
                scalar2=None,
                op0=ALU.mult,
            )

        def quantise(grouped, codes, scales):
            nc.vector.quantize_mx(
                out=codes.bitcast(FP8X4), scales=scales, in_=grouped[:].rearrange("p c t -> p (c t)")
            )

        def prepare_rf(blk):
            cols = slice(blk * BLOCK, (blk + 1) * BLOCK)
            quantise(regroup_by_words(loaded_rf[blk]), x_codes[RF][:, cols], x_scales[RF][:, cols])

        grouped_means = {}

        def prepare_bb_slab(blk, s):
            if s == 0:
                grouped = regroup.tile([P, BLOCK, PACK], BF16, align_bytes=64)
                grouped_means[blk] = grouped
            regroup_mean_slab(grouped_means[blk], *loaded_bb[blk], s)
            if s == SLABS - 1:
                cols = slice(blk * BLOCK, (blk + 1) * BLOCK)
                quantise(grouped_means[blk], x_codes[BB][:, cols], x_scales[BB][:, cols])
                if blk + AHEAD < BLOCKS:
                    load_rf(blk + AHEAD)
                    load_bb(blk + AHEAD)

        def product(blk, chunk, br):
            acc = products.tile([P, BLOCK], F32)
            n_cols = slice(chunk * P, (chunk + 1) * P)
            b_cols = slice(blk * BLOCK, (blk + 1) * BLOCK)
            nc.tensor.matmul_mx(
                out=acc[:],
                lhsT=w_codes[br][:, n_cols].bitcast(FP8X4),
                lhsT_scale=w_scales[br][:, n_cols],
                rhs=x_codes[br][:, b_cols].bitcast(FP8X4),
                rhs_scale=x_scales[br][:, b_cols],
                start=True,
                stop=True,
            )
            return acc

        staged = {}

        def sigmoid_step(blk, chunk, br):
            if br == RF:
                both = stage.tile([P, 2, BLOCK], F32)
                staged[(blk, chunk)] = both
            acc = product(blk, chunk, br)
            col = br * CHUNKS + chunk
            nc.scalar.activation(
                out=staged[(blk, chunk)][:, br, :], in_=acc[:], func=ACT.Sigmoid, bias=bias_neg[:, col : col + 1], scale=-1.0
            )

        def log_step(blk, chunk):
            flat = staged[(blk, chunk)][:].rearrange("p a b -> p (a b)")
            nc.scalar.activation(out=flat, in_=flat, func=ACT.Ln, bias=tiny[:, 0:1], scale=1.0)

        def tanh_step(blk, chunk):
            flat = staged[(blk, chunk)][:].rearrange("p a b -> p (a b)")
            nc.scalar.activation(out=flat, in_=flat, func=ACT.Tanh, scale=-1.0)

        def mish_step(blk, chunk, br):
            half = staged[(blk, chunk)][:, br, :]
            acc = product(blk, chunk, br)
            col = br * CHUNKS + chunk
            nc.vector.scalar_tensor_tensor(
                out=half, in0=acc[:], scalar=bias_pos[:, col : col + 1], in1=half, op0=ALU.add, op1=ALU.mult
            )

        def add_branches(blk, chunk):
            both = staged[(blk, chunk)]
            nc.gpsimd.tensor_tensor(out=both[:, RF, :], in0=both[:, RF, :], in1=both[:, BB, :], op=ALU.add)

        def transpose_back(blk, chunk, on_scalar):
            bank = back.tile([P, SLABS, P], F32)
            for s in range(SLABS):
                nc.tensor.transpose(bank[:, s, :], staged[(blk, chunk)][:, RF, s * P : (s + 1) * P], ident_f32[:])
            piece = result.tile([P, SLABS, P], F32)
            if on_scalar:
                nc.scalar.copy(out=piece[:], in_=bank[:])
            else:
                nc.vector.tensor_copy(out=piece[:], in_=bank[:])
            nc.sync.dma_start(
                out=out[blk * BLOCK : (blk + 1) * BLOCK, chunk * P : (chunk + 1) * P].rearrange("(s p) n -> p s n", p=P),
                in_=piece[:],
            )

        bias_rows = const.tile([P, P], BF16)
        nc.vector.memset(bias_rows[:], 0.0)
        nc.sync.dma_start(out=bias_rows[0:CHUNKS, :], in_=b_rfrf.rearrange("(c p) -> c p", p=P))
        nc.sync.dma_start(out=bias_rows[CHUNKS : 2 * CHUNKS, :], in_=b_bbrf.rearrange("(c p) -> c p", p=P))
        w_rf_rows = load_rows(W_rfrf)
        load_rf(0)
        w_bb_rows = load_rows(W_bbrf)
        load_bb(0)
        for blk in range(1, AHEAD):
            load_rf(blk)
            load_bb(blk)
        bias_bank = front.tile([P, P], BF16, tag="front")
        nc.tensor.transpose(bias_bank[:], bias_rows[:], ident_bf16[:])
        bias_pos = const.tile([P, 2 * CHUNKS], F32)
        nc.vector.tensor_copy(out=bias_pos[:], in_=bias_bank[:, 0 : 2 * CHUNKS])
        bias_neg = const.tile([P, 2 * CHUNKS], F32)
        nc.vector.tensor_scalar(
            out=bias_neg[:], in0=bias_bank[:, 0 : 2 * CHUNKS], scalar1=-1.0, scalar2=None, op0=ALU.mult
        )

        quantise(regroup_by_words(w_rf_rows), w_codes[RF][:], w_scales[RF][:])
        prepare_rf(0)
        for chunk in range(CHUNKS):
            sigmoid_step(0, chunk, RF)
        quantise(regroup_weights_by_quarters(w_bb_rows), w_codes[BB][:], w_scales[BB][:])
        for blk in range(BATCH + 1):
            if blk + 1 < BATCH:
                prepare_rf(blk + 1)
            for chunk in range(CHUNKS):
                if blk < BATCH:
                    prepare_bb_slab(blk, chunk)
                if blk + 1 < BATCH:
                    sigmoid_step(blk + 1, chunk, RF)
                if blk > 0:
                    sigmoid_step(blk - 1, chunk, BB)

        all_steps = [(blk, chunk) for blk in range(BLOCKS) for chunk in range(CHUNKS)]

        def trail(i, scalar_helps):
            if 0 <= i - LAG < len(all_steps):
                for br in BRANCHES:
                    mish_step(*all_steps[i - LAG], br)
                add_branches(*all_steps[i - LAG])
            if 0 <= i - LAG - BEHIND < len(all_steps):
                transpose_back(*all_steps[i - LAG - BEHIND], on_scalar=scalar_helps and i % 2 == 1)

        for batch in range(BATCHES):
            more = batch + 1 < BATCHES
            steps = range(batch * STEPS, (batch + 1) * STEPS)
            for i in steps:
                log_step(*all_steps[i])
            if more:
                for blk in range((batch + 1) * BATCH, (batch + 2) * BATCH):
                    prepare_rf(blk)
                    for s in range(SLABS):
                        prepare_bb_slab(blk, s)
            if more:
                for br in BRANCHES:
                    sigmoid_step(*all_steps[steps[0] + STEPS], br)
            for i in steps:
                tanh_step(*all_steps[i])
                if more and i < steps[-1]:
                    for br in BRANCHES:
                        sigmoid_step(*all_steps[i + 1 + STEPS], br)
                trail(i, scalar_helps=not more)
        for i in range(len(all_steps), len(all_steps) + LAG + BEHIND):
            trail(i, scalar_helps=True)
